import numpy as np
import ml_dtypes


def mxq(x, axis, fmt="e4m3"):
    dtype, down = {"e4m3": (ml_dtypes.float8_e4m3fn, 7), "e5m2": (ml_dtypes.float8_e5m2, 14)}[fmt]
    v = np.moveaxis(np.asarray(x, np.float32).astype(ml_dtypes.bfloat16).astype(np.float64), axis, -1)
    blocks = v.reshape(v.shape[:-1] + (-1, 32))
    amax = np.abs(blocks).max(-1, keepdims=True)
    byte = np.maximum(np.where(amax > 0, np.frexp(amax)[1] - 1 + 127, 0) - down, 1)
    scale = np.exp2(byte - 127.0)
    codes = (blocks / scale).astype(np.float32).astype(dtype).astype(np.float64)
    return np.moveaxis((codes * scale).reshape(v.shape), -1, axis)


WIDE = False


def mx_kscale(k):
    if not WIDE:
        return np.ones(k)
    levels = np.array([10, -10, 5, -5, 0])
    if k % 512:
        return np.exp2(np.random.permutation(np.resize(levels, k // 32))).repeat(32)
    a = np.empty((k // 512, 16))
    for p in range(k // 512):
        a[p, :8] = np.random.permutation(np.resize(levels, 8))
        for g in range(8):
            far = levels[np.abs(levels - a[p, g]) >= 10]
            a[p, g + 8] = far[np.random.randint(len(far))]
    return np.exp2(a.ravel()).repeat(32)


BF16 = ml_dtypes.bfloat16


def bf(x):
    return np.asarray(x, np.float32).astype(BF16)


def f64(x):
    return np.asarray(x).astype(np.float64)


B, D_IN, D_OUT = 4096, 512, 512


def sigmoid(v):
    return 1.0 / (1.0 + np.exp(-v))


def setup_inputs():
    s, t = mx_kscale(D_IN), mx_kscale(D_OUT)

    def wx():
        return bf(np.random.standard_normal((D_IN, D_OUT)) / np.sqrt(D_IN) / s[:, None])

    def wh():
        return bf(np.random.standard_normal((D_OUT, D_OUT)) / np.sqrt(D_OUT) / t[:, None])

    return {"x": bf(np.random.standard_normal((B, D_IN)) * s),
            "hist": bf(np.random.standard_normal((B, D_OUT)) * t),
            "Wix": wx(), "Wih": wh(), "b_i": bf(np.random.standard_normal(D_OUT) * 0.3),
            "Wcx": wx(), "Wch": wh(), "b_c": bf(np.random.standard_normal(D_OUT) * 0.3)}


def reference(x, hist, Wix, Wih, b_i, Wcx, Wch, b_c):
    xq = mxq(f64(x), 1, "e4m3")
    hq = mxq(f64(hist), 1, "e4m3")
    i = sigmoid((xq @ mxq(f64(Wix), 0, "e4m3")) + (hq @ mxq(f64(Wih), 0, "e4m3")) + f64(b_i))
    g = np.tanh((xq @ mxq(f64(Wcx), 0, "e4m3")) + (hq @ mxq(f64(Wch), 0, "e4m3")) + f64(b_c))
    return i * g

@@ -1,0 +1,248 @@
+from contextlib import ExitStack
+
+import concourse.mybir as mybir
+from concourse.masks import make_identity
+
+F32 = mybir.dt.float32
+BF16 = mybir.dt.bfloat16
+I32 = mybir.dt.int32
+U32 = mybir.dt.uint32
+U8 = mybir.dt.uint8
+FP8X4 = mybir.dt.float8_e4m3fn_x4
+ACT = mybir.ActivationFunctionType
+ALU = mybir.AluOpType
+
+P = 128
+B, D = 4096, 512
+GT = 4
+NG = B // (P * GT)
+NT = B // P
+FLOPS = 2 * B * D * D * 4
+
+CV = 336
+V_PRODUCTS = (30, 31)
+
+
+def tile_lstmmirrored_pa_t_kernel(tc, x, hist, Wix, Wih, b_i, Wcx, Wch, b_c, out):
+    nc = tc.nc
+    weights = (Wix, Wih, Wcx, Wch)
+    with ExitStack() as ctx:
+        const = ctx.enter_context(tc.tile_pool(name="const", bufs=1))
+        grp_pool = ctx.enter_context(tc.tile_pool(name="grp", bufs=2))
+        cod_pool = ctx.enter_context(tc.tile_pool(name="cod", bufs=3))
+        pre_pool = ctx.enter_context(tc.tile_pool(name="pre", bufs=4))
+        tg_pool = ctx.enter_context(tc.tile_pool(name="tg", bufs=6))
+        o_pool = ctx.enter_context(tc.tile_pool(name="o", bufs=4))
+        psum_t = ctx.enter_context(tc.psum_pool(name="pst", bufs=1))
+        psum_m = ctx.enter_context(tc.psum_pool(name="psm", bufs=1))
+        ctx.enter_context(tc.manual_schedule())
+
+        ident = const.tile([P, P], F32, name="ident")
+        ones = const.tile([P, P], BF16, name="ones")
+        brow = const.tile([P, 2 * D], BF16, name="brow")
+        bias = [const.tile([P, D], F32, name="bias%d" % q) for q in range(2)]
+        warm = const.tile([P, 8], F32, name="warm")
+        warm2 = const.tile([P, 8], F32, name="warm2")
+        wraw = [const.tile([P, 4, D], BF16, name="wraw%d" % k) for k in range(4)]
+        wgrp = [const.tile([P, 4 * D], BF16, name="wgrp%d" % k, align_bytes=64) for k in range(4)]
+        wcod = [const.tile([P, D], U32, name="wcod%d" % k, align_bytes=64) for k in range(4)]
+        wscl = [const.tile([P, D], U8, name="wscl%d" % k, align_bytes=64) for k in range(4)]
+        xs = [const.tile([P, GT, D], BF16, name="xs%d" % g) for g in range(NG)]
+        hs = [const.tile([P, GT, D], BF16, name="hs%d" % g) for g in range(NG)]
+
+        tps = {}
+        grps = {}
+        cods = {}
+        scls = {}
+        banks = {}
+        pres = {}
+        tgs = {}
+        outs = {}
+
+        nc.vector.memset(brow[:].bitcast(I32), 0)
+        nc.vector.memset(warm[:], 0.0)
+        nc.vector.memset(ones[:], 1.0)
+        make_identity(nc, ident[:])
+        nc.scalar.dma_start(out=brow[0:1, 0:D], in_=b_i.rearrange("(o n) -> o n", o=1))
+        nc.scalar.dma_start(out=brow[0:1, D:2 * D], in_=b_c.rearrange("(o n) -> o n", o=1))
+        nc.scalar.activation(out=warm2[:], in_=warm[:], func=ACT.Sigmoid)
+
+        def load_acts(g, j0, j1):
+            rows = slice(g * GT * P, (g + 1) * GT * P)
+            for dst, src in ((xs[g], x), (hs[g], hist)):
+                nc.sync.dma_start(out=dst[:, j0:j1, :], in_=src[rows, :].rearrange("(p t) k -> p t k", t=GT)[:, j0:j1, :])
+
+        def load_w(k):
+            nc.sync.dma_start(out=wraw[k][:], in_=weights[k].rearrange("(p t) c -> p t c", t=4))
+
+        load_w(0)
+        load_w(1)
+        load_acts(0, 0, 2)
+        load_w(2)
+        load_w(3)
+        load_acts(0, 2, 4)
+        for g in range(1, NG):
+            load_acts(g, 0, GT)
+
+        def transposes(n):
+            g, j = divmod(n, GT)
+            tp = psum_t.tile([P, 4 * P], F32, name="tp%d" % j, tag="tp%d" % j)
+            tps[n] = tp
+            for o, src in enumerate((xs[g], hs[g])):
+                words = src[:, j, :].bitcast(F32)
+                for u in range(2):
+                    c = (2 * o + u) * P
+                    nc.tensor.transpose(tp[:, c:c + P], words[:, u:2 * P:2], ident[:])
+
+        def leave(n, on_vector):
+            g, j = divmod(n, GT)
+            if g not in grps:
+                grps[g] = grp_pool.tile([P, GT * 1024], BF16, name="grp", tag="grp", align_bytes=64)
+            dst = grps[g][:, j * 1024:(j + 1) * 1024].bitcast(F32).rearrange("p (o b u) -> p o b u", o=2, u=2)
+            src = tps[n][:].rearrange("p (o u b) -> p o b u", o=2, u=2)
+            if on_vector:
+                nc.vector.tensor_copy(out=dst, in_=src)
+            else:
+                nc.scalar.copy(out=dst, in_=src)
+
+        def quantise(g, j0, j1):
+            if g not in cods:
+                cods[g] = cod_pool.tile([P, GT * 256], U32, name="cod", tag="cod", align_bytes=64)
+                scls[g] = cod_pool.tile([P, GT * 256], U8, name="scl", tag="scl", align_bytes=64)
+            nc.vector.quantize_mx(
+                out=cods[g][:, j0 * 256:j1 * 256].bitcast(FP8X4),
+                scales=scls[g][:, j0 * 256:j1 * 256],
+                in_=grps[g][:, j0 * 1024:j1 * 1024],
+            )
+
+        def regroup_w(k):
+            for c0, c1, on_vector in ((0, CV, True), (CV, D, False)):
+                dst = wgrp[k][:, 4 * c0:4 * c1].rearrange("p (c i t) -> p c t i", i=4, t=4)
+                src = wraw[k][:, :, c0:c1].rearrange("p t (c i) -> p c t i", i=4)
+                if on_vector:
+                    nc.vector.tensor_copy(out=dst, in_=src)
+                else:
+                    nc.scalar.copy(out=dst, in_=src)
+
+        def quantise_w(k):
+            nc.vector.quantize_mx(out=wcod[k][:].bitcast(FP8X4), scales=wscl[k][:], in_=wgrp[k][:])
+
+        def open_banks(t):
+            banks[t] = [
+                psum_m.tile([P, D], F32, name="m%s%d" % (s, t % 2), tag="m%s%d" % (s, t % 2)) for s in ("i", "g")
+            ]
+
+        def mx_pass(t, k):
+            g, j = divmod(t, GT)
+            c = j * 256 + (k % 2) * P
+            nc.tensor.matmul_mx(
+                out=banks[t][k // 2][:],
+                lhsT=cods[g][:, c:c + P].bitcast(FP8X4),
+                lhsT_scale=scls[g][:, c:c + P],
+                rhs=wcod[k][:].bitcast(FP8X4),
+                rhs_scale=wscl[k][:],
+                start=(k % 2 == 0),
+                stop=(k % 2 == 1),
+            )
+
+        def add_bias(t, q):
+            a = pre_pool.tile([P, D], F32, name="a%d" % q, tag="a%d" % q)
+            pres[(t, q)] = a
+            nc.vector.tensor_tensor(out=a[:], in0=banks[t][q][:], in1=bias[q][:], op=ALU.add)
+
+        def gate(t, q):
+            g, j = divmod(t, GT)
+            if q == 0:
+                if g not in outs:
+                    outs[g] = o_pool.tile([P, GT, D], F32, name="o", tag="o")
+                nc.scalar.activation(out=outs[g][:, j, :], in_=pres[(t, 0)][:], func=ACT.Sigmoid)
+            else:
+                tgs[t] = tg_pool.tile([P, D], F32, name="tg", tag="tg")
+                nc.scalar.activation(out=tgs[t][:], in_=pres[(t, 1)][:], func=ACT.Tanh)
+
+        def product_and_store(t):
+            g, j = divmod(t, GT)
+            eng = nc.vector if t in V_PRODUCTS else nc.gpsimd
+            eng.tensor_tensor(out=outs[g][:, j, :], in0=outs[g][:, j, :], in1=tgs[t][:], op=ALU.mult)
+            view = out[g * GT * P:(g + 1) * GT * P, :].rearrange("(p t) d -> p t d", t=GT)
+            if g == NG - 1:
+                nc.sync.dma_start(out=view[:, j, :], in_=outs[g][:, j, :])
+            elif j == GT - 1:
+                nc.sync.dma_start(out=view, in_=outs[g][:])
+
+        regroup_w(0)
+        regroup_w(1)
+        transposes(0)
+        transposes(1)
+        leave(0, False)
+        leave(1, False)
+        quantise_w(0)
+        quantise_w(1)
+        regroup_w(2)
+        quantise(0, 0, 2)
+        bbs = []
+        for q in range(2):
+            bb = psum_t.tile([P, D], F32, name="bb%d" % q, tag="tp%d" % q)
+            bbs.append(bb)
+            nc.tensor.matmul(out=bb[:], lhsT=ones[:], rhs=brow[:, q * D:(q + 1) * D], start=True, stop=True)
+        open_banks(0)
+        open_banks(1)
+        for k in range(2):
+            mx_pass(0, k)
+            mx_pass(1, k)
+        regroup_w(3)
+        for q in range(2):
+            nc.scalar.copy(out=bias[q][:], in_=bbs[q][:])
+        transposes(2)
+        transposes(3)
+        for k in range(2, 4):
+            quantise_w(k)
+            mx_pass(0, k)
+            mx_pass(1, k)
+        leave(2, False)
+        leave(3, False)
+        add_bias(0, 0)
+        add_bias(1, 0)
+        quantise(0, 2, 4)
+        add_bias(0, 1)
+        add_bias(1, 1)
+        gate(0, 0)
+        gate(1, 0)
+        gate(0, 1)
+        gate(1, 1)
+        product_and_store(0)
+        product_and_store(1)
+        for n in range(4, 8):
+            transposes(n)
+
+        for t in range(2, NT):
+            g, j = divmod(t, GT)
+            nxt = (g + 1) * GT
+            more = g > 0 and nxt < NT
+            if j == 0 and more:
+                for n in range(nxt, nxt + GT):
+                    transposes(n)
+            open_banks(t)
+            for k in range(4):
+                mx_pass(t, k)
+            if t == 2:
+                leave(4, True)
+                leave(5, False)
+                leave(6, False)
+                leave(7, False)
+            if j == 0 and more:
+                leave(nxt, True)
+                leave(nxt + 1, False)
+            if j == 1 and more:
+                leave(nxt + 2, False)
+                leave(nxt + 3, False)
+            add_bias(t, 0)
+            add_bias(t, 1)
+            if t == 3 or (j == 2 and more):
+                quantise(g + 1, 0, GT)
+            gate(t, 0)
+            gate(t, 1)
+            if t not in V_PRODUCTS:
+                product_and_store(t)
+        for t in V_PRODUCTS:
+            product_and_store(t)

@@ -21,6 +21,7 @@ FLOPS = 2 * B * D * D * 4
 
 CV = 336
 V_PRODUCTS = (30, 31)
+NB = 4
 
 
 def tile_lstmmirrored_pa_t_kernel(tc, x, hist, Wix, Wih, b_i, Wcx, Wch, b_c, out):
@@ -33,14 +34,13 @@ def tile_lstmmirrored_pa_t_kernel(tc, x, hist, Wix, Wih, b_i, Wcx, Wch, b_c, out
         pre_pool = ctx.enter_context(tc.tile_pool(name="pre", bufs=4))
         tg_pool = ctx.enter_context(tc.tile_pool(name="tg", bufs=6))
         o_pool = ctx.enter_context(tc.tile_pool(name="o", bufs=4))
-        psum_t = ctx.enter_context(tc.psum_pool(name="pst", bufs=1))
-        psum_m = ctx.enter_context(tc.psum_pool(name="psm", bufs=1))
+        psum = ctx.enter_context(tc.psum_pool(name="ps", bufs=1))
         ctx.enter_context(tc.manual_schedule())
 
         ident = const.tile([P, P], F32, name="ident")
         ones = const.tile([P, P], BF16, name="ones")
         brow = const.tile([P, 2 * D], BF16, name="brow")
-        bias = [const.tile([P, D], F32, name="bias%d" % q) for q in range(2)]
+        bias = const.tile([P, 2 * D], BF16, name="bias")
         warm = const.tile([P, 8], F32, name="warm")
         warm2 = const.tile([P, 8], F32, name="warm2")
         wraw = [const.tile([P, 4, D], BF16, name="wraw%d" % k) for k in range(4)]
@@ -59,14 +59,6 @@ def tile_lstmmirrored_pa_t_kernel(tc, x, hist, Wix, Wih, b_i, Wcx, Wch, b_c, out
         tgs = {}
         outs = {}
 
-        nc.vector.memset(brow[:].bitcast(I32), 0)
-        nc.vector.memset(warm[:], 0.0)
-        nc.vector.memset(ones[:], 1.0)
-        make_identity(nc, ident[:])
-        nc.scalar.dma_start(out=brow[0:1, 0:D], in_=b_i.rearrange("(o n) -> o n", o=1))
-        nc.scalar.dma_start(out=brow[0:1, D:2 * D], in_=b_c.rearrange("(o n) -> o n", o=1))
-        nc.scalar.activation(out=warm2[:], in_=warm[:], func=ACT.Sigmoid)
-
         def load_acts(g, j0, j1):
             rows = slice(g * GT * P, (g + 1) * GT * P)
             for dst, src in ((xs[g], x), (hs[g], hist)):
@@ -75,18 +67,9 @@ def tile_lstmmirrored_pa_t_kernel(tc, x, hist, Wix, Wih, b_i, Wcx, Wch, b_c, out
         def load_w(k):
             nc.sync.dma_start(out=wraw[k][:], in_=weights[k].rearrange("(p t) c -> p t c", t=4))
 
-        load_w(0)
-        load_w(1)
-        load_acts(0, 0, 2)
-        load_w(2)
-        load_w(3)
-        load_acts(0, 2, 4)
-        for g in range(1, NG):
-            load_acts(g, 0, GT)
-
         def transposes(n):
             g, j = divmod(n, GT)
-            tp = psum_t.tile([P, 4 * P], F32, name="tp%d" % j, tag="tp%d" % j)
+            tp = psum.tile([P, 4 * P], F32, name="tp%d" % j, tag="tp%d" % j)
             tps[n] = tp
             for o, src in enumerate((xs[g], hs[g])):
                 words = src[:, j, :].bitcast(F32)
@@ -115,8 +98,8 @@ def tile_lstmmirrored_pa_t_kernel(tc, x, hist, Wix, Wih, b_i, Wcx, Wch, b_c, out
                 in_=grps[g][:, j0 * 1024:j1 * 1024],
             )
 
-        def regroup_w(k):
-            for c0, c1, on_vector in ((0, CV, True), (CV, D, False)):
+        def regroup_w(k, cv=CV):
+            for c0, c1, on_vector in ((0, cv, True), (cv, D, False)):
                 dst = wgrp[k][:, 4 * c0:4 * c1].rearrange("p (c i t) -> p c t i", i=4, t=4)
                 src = wraw[k][:, :, c0:c1].rearrange("p t (c i) -> p c t i", i=4)
                 if on_vector:
@@ -127,28 +110,28 @@ def tile_lstmmirrored_pa_t_kernel(tc, x, hist, Wix, Wih, b_i, Wcx, Wch, b_c, out
         def quantise_w(k):
             nc.vector.quantize_mx(out=wcod[k][:].bitcast(FP8X4), scales=wscl[k][:], in_=wgrp[k][:])
 
-        def open_banks(t):
-            banks[t] = [
-                psum_m.tile([P, D], F32, name="m%s%d" % (s, t % 2), tag="m%s%d" % (s, t % 2)) for s in ("i", "g")
-            ]
-
-        def mx_pass(t, k):
+        def mx(t, q):
             g, j = divmod(t, GT)
-            c = j * 256 + (k % 2) * P
-            nc.tensor.matmul_mx(
-                out=banks[t][k // 2][:],
-                lhsT=cods[g][:, c:c + P].bitcast(FP8X4),
-                lhsT_scale=scls[g][:, c:c + P],
-                rhs=wcod[k][:].bitcast(FP8X4),
-                rhs_scale=wscl[k][:],
-                start=(k % 2 == 0),
-                stop=(k % 2 == 1),
-            )
+            r = len(banks)
+            bank = psum.tile([P, D], F32, name="m%d" % (r % NB), tag="m%d" % (r % NB))
+            banks[(t, q)] = bank
+            for s in range(2):
+                c = j * 256 + s * P
+                k = 2 * q + s
+                nc.tensor.matmul_mx(
+                    out=bank[:],
+                    lhsT=cods[g][:, c:c + P].bitcast(FP8X4),
+                    lhsT_scale=scls[g][:, c:c + P],
+                    rhs=wcod[k][:].bitcast(FP8X4),
+                    rhs_scale=wscl[k][:],
+                    start=(s == 0),
+                    stop=(s == 1),
+                )
 
         def add_bias(t, q):
             a = pre_pool.tile([P, D], F32, name="a%d" % q, tag="a%d" % q)
             pres[(t, q)] = a
-            nc.vector.tensor_tensor(out=a[:], in0=banks[t][q][:], in1=bias[q][:], op=ALU.add)
+            nc.vector.tensor_tensor(out=a[:], in0=banks[(t, q)][:], in1=bias[:, q * D:(q + 1) * D], op=ALU.add)
 
         def gate(t, q):
             g, j = divmod(t, GT)
@@ -170,66 +153,91 @@ def tile_lstmmirrored_pa_t_kernel(tc, x, hist, Wix, Wih, b_i, Wcx, Wch, b_c, out
             elif j == GT - 1:
                 nc.sync.dma_start(out=view, in_=outs[g][:])
 
+        nc.vector.memset(brow[:].bitcast(I32), 0)
+        nc.vector.memset(warm[:], 0.0)
+        nc.vector.memset(ones[:], 1.0)
+        make_identity(nc, ident[:])
+        nc.scalar.activation(out=warm2[:], in_=warm[:], func=ACT.Sigmoid)
+        load_w(0)
+        load_acts(0, 0, 2)
+        nc.sync.dma_start(out=brow[0:1, 0:D], in_=b_i.rearrange("(o n) -> o n", o=1))
+        nc.sync.dma_start(out=brow[0:1, D:2 * D], in_=b_c.rearrange("(o n) -> o n", o=1))
+        load_w(1)
+        load_acts(0, 2, 4)
+        load_w(2)
+        load_acts(1, 0, 2)
+        load_w(3)
+        load_acts(1, 2, 4)
+        for g in range(2, NG):
+            load_acts(g, 0, GT)
+
         regroup_w(0)
-        regroup_w(1)
         transposes(0)
         transposes(1)
+        quantise_w(0)
         leave(0, False)
         leave(1, False)
-        quantise_w(0)
-        quantise_w(1)
-        regroup_w(2)
+        regroup_w(1)
         quantise(0, 0, 2)
-        bbs = []
-        for q in range(2):
-            bb = psum_t.tile([P, D], F32, name="bb%d" % q, tag="tp%d" % q)
-            bbs.append(bb)
-            nc.tensor.matmul(out=bb[:], lhsT=ones[:], rhs=brow[:, q * D:(q + 1) * D], start=True, stop=True)
-        open_banks(0)
-        open_banks(1)
-        for k in range(2):
-            mx_pass(0, k)
-            mx_pass(1, k)
-        regroup_w(3)
-        for q in range(2):
-            nc.scalar.copy(out=bias[q][:], in_=bbs[q][:])
+        quantise_w(1)
         transposes(2)
         transposes(3)
-        for k in range(2, 4):
-            quantise_w(k)
-            mx_pass(0, k)
-            mx_pass(1, k)
+        mx(0, 0)
+        mx(1, 0)
         leave(2, False)
-        leave(3, False)
-        add_bias(0, 0)
-        add_bias(1, 0)
+        leave(3, True)
+        regroup_w(2)
+        bb = psum.tile([P, 2 * D], BF16, name="bb", tag="tp0")
+        for q in range(2):
+            nc.tensor.matmul(out=bb[:, q * D:(q + 1) * D], lhsT=ones[:], rhs=brow[:, q * D:(q + 1) * D], start=True, stop=True)
+        nc.scalar.copy(out=bias[:], in_=bb[:])
         quantise(0, 2, 4)
-        add_bias(0, 1)
-        add_bias(1, 1)
+        mx(2, 0)
+        mx(3, 0)
+        quantise_w(2)
+        add_bias(0, 0)
+        regroup_w(3)
+        add_bias(1, 0)
         gate(0, 0)
-        gate(1, 0)
-        gate(0, 1)
-        gate(1, 1)
-        product_and_store(0)
-        product_and_store(1)
+        quantise_w(3)
         for n in range(4, 8):
             transposes(n)
+        mx(0, 1)
+        add_bias(2, 0)
+        mx(1, 1)
+        add_bias(3, 0)
+        mx(2, 1)
+        mx(3, 1)
+        leave(4, False)
+        leave(5, False)
+        gate(1, 0)
+        add_bias(0, 1)
+        leave(6, False)
+        gate(0, 1)
+        product_and_store(0)
+        leave(7, True)
+        add_bias(1, 1)
+        gate(2, 0)
+        gate(1, 1)
+        product_and_store(1)
+        add_bias(2, 1)
+        quantise(1, 0, 4)
+        add_bias(3, 1)
+        gate(2, 1)
+        product_and_store(2)
+        gate(3, 0)
+        gate(3, 1)
+        product_and_store(3)
 
-        for t in range(2, NT):
+        for t in range(4, NT):
             g, j = divmod(t, GT)
             nxt = (g + 1) * GT
-            more = g > 0 and nxt < NT
+            more = nxt < NT
             if j == 0 and more:
                 for n in range(nxt, nxt + GT):
                     transposes(n)
-            open_banks(t)
-            for k in range(4):
-                mx_pass(t, k)
-            if t == 2:
-                leave(4, True)
-                leave(5, False)
-                leave(6, False)
-                leave(7, False)
+            mx(t, 0)
+            mx(t, 1)
             if j == 0 and more:
                 leave(nxt, True)
                 leave(nxt + 1, False)
@@ -238,7 +246,7 @@ def tile_lstmmirrored_pa_t_kernel(tc, x, hist, Wix, Wih, b_i, Wcx, Wch, b_c, out
                 leave(nxt + 3, False)
             add_bias(t, 0)
             add_bias(t, 1)
-            if t == 3 or (j == 2 and more):
+            if j == 2 and more:
                 quantise(g + 1, 0, GT)
             gate(t, 0)
             gate(t, 1)

@@ -110,48 +110,64 @@ def tile_lstmmirrored_pa_t_kernel(tc, x, hist, Wix, Wih, b_i, Wcx, Wch, b_c, out
         def quantise_w(k):
             nc.vector.quantize_mx(out=wcod[k][:].bitcast(FP8X4), scales=wscl[k][:], in_=wgrp[k][:])
 
-        def mx(t, q):
+        def mx(t, q, cols=(0, D)):
             g, j = divmod(t, GT)
-            r = len(banks)
-            bank = psum.tile([P, D], F32, name="m%d" % (r % NB), tag="m%d" % (r % NB))
-            banks[(t, q)] = bank
+            c0, c1 = cols
+            if c0 == 0:
+                r = len(banks)
+                banks[(t, q)] = psum.tile([P, D], F32, name="m%d" % (r % NB), tag="m%d" % (r % NB))
             for s in range(2):
                 c = j * 256 + s * P
                 k = 2 * q + s
                 nc.tensor.matmul_mx(
-                    out=bank[:],
+                    out=banks[(t, q)][:, c0:c1],
                     lhsT=cods[g][:, c:c + P].bitcast(FP8X4),
                     lhsT_scale=scls[g][:, c:c + P],
-                    rhs=wcod[k][:].bitcast(FP8X4),
-                    rhs_scale=wscl[k][:],
+                    rhs=wcod[k][:, c0:c1].bitcast(FP8X4),
+                    rhs_scale=wscl[k][:, c0:c1],
                     start=(s == 0),
                     stop=(s == 1),
                 )
 
-        def add_bias(t, q):
-            a = pre_pool.tile([P, D], F32, name="a%d" % q, tag="a%d" % q)
-            pres[(t, q)] = a
-            nc.vector.tensor_tensor(out=a[:], in0=banks[(t, q)][:], in1=bias[:, q * D:(q + 1) * D], op=ALU.add)
+        def add_bias(t, q, cols=(0, D)):
+            c0, c1 = cols
+            if c0 == 0:
+                pres[(t, q)] = pre_pool.tile([P, D], F32, name="a%d" % q, tag="a%d" % q)
+            nc.vector.tensor_tensor(
+                out=pres[(t, q)][:, c0:c1], in0=banks[(t, q)][:, c0:c1], in1=bias[:, q * D + c0:q * D + c1], op=ALU.add
+            )
 
-        def gate(t, q):
+        def gate(t, q, cols=(0, D)):
             g, j = divmod(t, GT)
+            c0, c1 = cols
             if q == 0:
                 if g not in outs:
                     outs[g] = o_pool.tile([P, GT, D], F32, name="o", tag="o")
-                nc.scalar.activation(out=outs[g][:, j, :], in_=pres[(t, 0)][:], func=ACT.Sigmoid)
+                nc.scalar.activation(out=outs[g][:, j, c0:c1], in_=pres[(t, 0)][:, c0:c1], func=ACT.Sigmoid)
             else:
-                tgs[t] = tg_pool.tile([P, D], F32, name="tg", tag="tg")
-                nc.scalar.activation(out=tgs[t][:], in_=pres[(t, 1)][:], func=ACT.Tanh)
+                if c0 == 0:
+                    tgs[t] = tg_pool.tile([P, D], F32, name="tg", tag="tg")
+                nc.scalar.activation(out=tgs[t][:, c0:c1], in_=pres[(t, 1)][:, c0:c1], func=ACT.Tanh)
+
+        def product(t, cols=(0, D)):
+            g, j = divmod(t, GT)
+            c0, c1 = cols
+            eng = nc.vector if t in V_PRODUCTS else nc.gpsimd
+            o = outs[g][:, j, c0:c1]
+            eng.tensor_tensor(out=o, in0=o, in1=tgs[t][:, c0:c1], op=ALU.mult)
+
+        def store(g, j0, j1, cols=(0, D)):
+            c0, c1 = cols
+            view = out[g * GT * P:(g + 1) * GT * P, :].rearrange("(p t) d -> p t d", t=GT)
+            nc.sync.dma_start(out=view[:, j0:j1, c0:c1], in_=outs[g][:, j0:j1, c0:c1])
 
         def product_and_store(t):
             g, j = divmod(t, GT)
-            eng = nc.vector if t in V_PRODUCTS else nc.gpsimd
-            eng.tensor_tensor(out=outs[g][:, j, :], in0=outs[g][:, j, :], in1=tgs[t][:], op=ALU.mult)
-            view = out[g * GT * P:(g + 1) * GT * P, :].rearrange("(p t) d -> p t d", t=GT)
+            product(t)
             if g == NG - 1:
-                nc.sync.dma_start(out=view[:, j, :], in_=outs[g][:, j, :])
-            elif j == GT - 1:
-                nc.sync.dma_start(out=view, in_=outs[g][:])
+                store(g, j, j + 1)
+            elif j % 2 == 1:
+                store(g, j - 1, j + 1)
 
         nc.vector.memset(brow[:].bitcast(I32), 0)
         nc.vector.memset(warm[:], 0.0)
@@ -203,33 +219,31 @@ def tile_lstmmirrored_pa_t_kernel(tc, x, hist, Wix, Wih, b_i, Wcx, Wch, b_c, out
         for n in range(4, 8):
             transposes(n)
         mx(0, 1)
-        add_bias(2, 0)
         mx(1, 1)
-        add_bias(3, 0)
-        mx(2, 1)
-        mx(3, 1)
         leave(4, False)
         leave(5, False)
-        gate(1, 0)
-        add_bias(0, 1)
         leave(6, False)
-        gate(0, 1)
-        product_and_store(0)
-        leave(7, True)
-        add_bias(1, 1)
+        add_bias(2, 0)
+        gate(1, 0)
+        mx(2, 1)
+        add_bias(3, 0)
         gate(2, 0)
+        mx(3, 1)
+        leave(7, True)
+        add_bias(0, 1)
+        gate(0, 1)
+        quantise(1, 0, 4)
+        product_and_store(0)
+        gate(3, 0)
+        add_bias(1, 1)
         gate(1, 1)
         product_and_store(1)
-        add_bias(2, 1)
-        quantise(1, 0, 4)
-        add_bias(3, 1)
-        gate(2, 1)
-        product_and_store(2)
-        gate(3, 0)
-        gate(3, 1)
-        product_and_store(3)
+        for t in (2, 3):
+            add_bias(t, 1)
+            gate(t, 1)
+            product_and_store(t)
 
-        for t in range(4, NT):
+        for t in range(4, NT - 1):
             g, j = divmod(t, GT)
             nxt = (g + 1) * GT
             more = nxt < NT
@@ -250,7 +264,20 @@ def tile_lstmmirrored_pa_t_kernel(tc, x, hist, Wix, Wih, b_i, Wcx, Wch, b_c, out
                 quantise(g + 1, 0, GT)
             gate(t, 0)
             gate(t, 1)
-            if t not in V_PRODUCTS:
+            if t < NT - 2:
                 product_and_store(t)
-        for t in V_PRODUCTS:
-            product_and_store(t)
+
+        t = NT - 1
+        halves = ((0, D // 2), (D // 2, D))
+        mx(t, 0)
+        for cols in halves:
+            mx(t, 1, cols)
+        add_bias(t, 0)
+        gate(t, 0)
+        for cols in halves:
+            add_bias(t, 1, cols)
+        product_and_store(t - 1)
+        for cols in halves:
+            gate(t, 1, cols)
+            product(t, cols)
+            store(NG - 1, GT - 1, GT, cols)

@@ -44,9 +44,9 @@ def tile_lstmmirrored_pa_t_kernel(tc, x, hist, Wix, Wih, b_i, Wcx, Wch, b_c, out
         warm = const.tile([P, 8], F32, name="warm")
         warm2 = const.tile([P, 8], F32, name="warm2")
         wraw = [const.tile([P, 4, D], BF16, name="wraw%d" % k) for k in range(4)]
-        wgrp = [const.tile([P, 4 * D], BF16, name="wgrp%d" % k, align_bytes=64) for k in range(4)]
-        wcod = [const.tile([P, D], U32, name="wcod%d" % k, align_bytes=64) for k in range(4)]
-        wscl = [const.tile([P, D], U8, name="wscl%d" % k, align_bytes=64) for k in range(4)]
+        wgrp = [const.tile([P, 4 * D], BF16, name="wgrp%d" % k, align_bytes=256) for k in range(4)]
+        wcod = [const.tile([P, D], U32, name="wcod%d" % k, align_bytes=256) for k in range(4)]
+        wscl = [const.tile([P, D], U8, name="wscl%d" % k, align_bytes=256) for k in range(4)]
         xs = [const.tile([P, GT, D], BF16, name="xs%d" % g) for g in range(NG)]
         hs = [const.tile([P, GT, D], BF16, name="hs%d" % g) for g in range(NG)]
 
@@ -80,7 +80,7 @@ def tile_lstmmirrored_pa_t_kernel(tc, x, hist, Wix, Wih, b_i, Wcx, Wch, b_c, out
         def leave(n, on_vector):
             g, j = divmod(n, GT)
             if g not in grps:
-                grps[g] = grp_pool.tile([P, GT * 1024], BF16, name="grp", tag="grp", align_bytes=64)
+                grps[g] = grp_pool.tile([P, GT * 1024], BF16, name="grp", tag="grp", align_bytes=256)
             dst = grps[g][:, j * 1024:(j + 1) * 1024].bitcast(F32).rearrange("p (o b u) -> p o b u", o=2, u=2)
             src = tps[n][:].rearrange("p (o u b) -> p o b u", o=2, u=2)
             if on_vector:
@@ -90,8 +90,8 @@ def tile_lstmmirrored_pa_t_kernel(tc, x, hist, Wix, Wih, b_i, Wcx, Wch, b_c, out
 
         def quantise(g, j0, j1):
             if g not in cods:
-                cods[g] = cod_pool.tile([P, GT * 256], U32, name="cod", tag="cod", align_bytes=64)
-                scls[g] = cod_pool.tile([P, GT * 256], U8, name="scl", tag="scl", align_bytes=64)
+                cods[g] = cod_pool.tile([P, GT * 256], U32, name="cod", tag="cod", align_bytes=256)
+                scls[g] = cod_pool.tile([P, GT * 256], U8, name="scl", tag="scl", align_bytes=256)
             nc.vector.quantize_mx(
                 out=cods[g][:, j0 * 256:j1 * 256].bitcast(FP8X4),
                 scales=scls[g][:, j0 * 256:j1 * 256],
@@ -169,15 +169,16 @@ def tile_lstmmirrored_pa_t_kernel(tc, x, hist, Wix, Wih, b_i, Wcx, Wch, b_c, out
             elif j % 2 == 1:
                 store(g, j - 1, j + 1)
 
+        nc.vector.memset(ident[:], 0.0)
+        make_identity(nc, ident[:], nomemset=True)
         nc.vector.memset(brow[:].bitcast(I32), 0)
         nc.vector.memset(warm[:], 0.0)
         nc.vector.memset(ones[:], 1.0)
-        make_identity(nc, ident[:])
+        nc.scalar.dma_start(out=brow[0:1, 0:D], in_=b_i.rearrange("(o n) -> o n", o=1))
+        nc.scalar.dma_start(out=brow[0:1, D:2 * D], in_=b_c.rearrange("(o n) -> o n", o=1))
         nc.scalar.activation(out=warm2[:], in_=warm[:], func=ACT.Sigmoid)
         load_w(0)
         load_acts(0, 0, 2)
-        nc.sync.dma_start(out=brow[0:1, 0:D], in_=b_i.rearrange("(o n) -> o n", o=1))
-        nc.sync.dma_start(out=brow[0:1, D:2 * D], in_=b_c.rearrange("(o n) -> o n", o=1))
         load_w(1)
         load_acts(0, 2, 4)
         load_w(2)
@@ -190,6 +191,9 @@ def tile_lstmmirrored_pa_t_kernel(tc, x, hist, Wix, Wih, b_i, Wcx, Wch, b_c, out
         regroup_w(0)
         transposes(0)
         transposes(1)
+        bb = psum.tile([P, 2 * D], BF16, name="bb", tag="m3")
+        for q in range(2):
+            nc.tensor.matmul(out=bb[:, q * D:(q + 1) * D], lhsT=ones[:], rhs=brow[:, q * D:(q + 1) * D], start=True, stop=True)
         quantise_w(0)
         leave(0, False)
         leave(1, False)
@@ -202,11 +206,8 @@ def tile_lstmmirrored_pa_t_kernel(tc, x, hist, Wix, Wih, b_i, Wcx, Wch, b_c, out
         mx(1, 0)
         leave(2, False)
         leave(3, True)
-        regroup_w(2)
-        bb = psum.tile([P, 2 * D], BF16, name="bb", tag="tp0")
-        for q in range(2):
-            nc.tensor.matmul(out=bb[:, q * D:(q + 1) * D], lhsT=ones[:], rhs=brow[:, q * D:(q + 1) * D], start=True, stop=True)
         nc.scalar.copy(out=bias[:], in_=bb[:])
+        regroup_w(2)
         quantise(0, 2, 4)
         mx(2, 0)
         mx(3, 0)

@@ -254,14 +254,13 @@ def tile_lstmmirrored_pa_t_kernel(tc, x, hist, Wix, Wih, b_i, Wcx, Wch, b_c, out
             mx(t, 0)
             mx(t, 1)
             if j == 0 and more:
-                leave(nxt, True)
+                leave(nxt + 0, True)
                 leave(nxt + 1, False)
-            if j == 1 and more:
                 leave(nxt + 2, False)
                 leave(nxt + 3, False)
             add_bias(t, 0)
             add_bias(t, 1)
-            if j == 2 and more:
+            if j == 1 and more:
                 quantise(g + 1, 0, GT)
             gate(t, 0)
             gate(t, 1)

@@ -206,9 +206,11 @@ def tile_lstmmirrored_pa_t_kernel(tc, x, hist, Wix, Wih, b_i, Wcx, Wch, b_c, out
         mx(1, 0)
         leave(2, False)
         leave(3, True)
-        nc.scalar.copy(out=bias[:], in_=bb[:])
         regroup_w(2)
+        nc.scalar.copy(out=bias[:], in_=bb[:])
         quantise(0, 2, 4)
+        transposes(4)
+        transposes(5)
         mx(2, 0)
         mx(3, 0)
         quantise_w(2)
@@ -217,8 +219,8 @@ def tile_lstmmirrored_pa_t_kernel(tc, x, hist, Wix, Wih, b_i, Wcx, Wch, b_c, out
         add_bias(1, 0)
         gate(0, 0)
         quantise_w(3)
-        for n in range(4, 8):
-            transposes(n)
+        transposes(6)
+        transposes(7)
         mx(0, 1)
         mx(1, 1)
         leave(4, False)

from contextlib import ExitStack

import concourse.mybir as mybir
from concourse.masks import make_identity

F32 = mybir.dt.float32
BF16 = mybir.dt.bfloat16
I32 = mybir.dt.int32
U32 = mybir.dt.uint32
U8 = mybir.dt.uint8
FP8X4 = mybir.dt.float8_e4m3fn_x4
ACT = mybir.ActivationFunctionType
ALU = mybir.AluOpType

P = 128
B, D = 4096, 512
GT = 4
NG = B // (P * GT)
NT = B // P
FLOPS = 2 * B * D * D * 4

CV = 336
V_PRODUCTS = (30, 31)
NB = 4


def tile_lstmmirrored_pa_t_kernel(tc, x, hist, Wix, Wih, b_i, Wcx, Wch, b_c, out):
    nc = tc.nc
    weights = (Wix, Wih, Wcx, Wch)
    with ExitStack() as ctx:
        const = ctx.enter_context(tc.tile_pool(name="const", bufs=1))
        grp_pool = ctx.enter_context(tc.tile_pool(name="grp", bufs=2))
        cod_pool = ctx.enter_context(tc.tile_pool(name="cod", bufs=3))
        pre_pool = ctx.enter_context(tc.tile_pool(name="pre", bufs=4))
        tg_pool = ctx.enter_context(tc.tile_pool(name="tg", bufs=6))
        o_pool = ctx.enter_context(tc.tile_pool(name="o", bufs=4))
        psum = ctx.enter_context(tc.psum_pool(name="ps", bufs=1))
        ctx.enter_context(tc.manual_schedule())

        ident = const.tile([P, P], F32, name="ident")
        ones = const.tile([P, P], BF16, name="ones")
        brow = const.tile([P, 2 * D], BF16, name="brow")
        bias = const.tile([P, 2 * D], BF16, name="bias")
        warm = const.tile([P, 8], F32, name="warm")
        warm2 = const.tile([P, 8], F32, name="warm2")
        wraw = [const.tile([P, 4, D], BF16, name="wraw%d" % k) for k in range(4)]
        wgrp = [const.tile([P, 4 * D], BF16, name="wgrp%d" % k, align_bytes=256) for k in range(4)]
        wcod = [const.tile([P, D], U32, name="wcod%d" % k, align_bytes=256) for k in range(4)]
        wscl = [const.tile([P, D], U8, name="wscl%d" % k, align_bytes=256) for k in range(4)]
        xs = [const.tile([P, GT, D], BF16, name="xs%d" % g) for g in range(NG)]
        hs = [const.tile([P, GT, D], BF16, name="hs%d" % g) for g in range(NG)]

        tps = {}
        grps = {}
        cods = {}
        scls = {}
        banks = {}
        pres = {}
        tgs = {}
        outs = {}

        def load_acts(g, j0, j1):
            rows = slice(g * GT * P, (g + 1) * GT * P)
            for dst, src in ((xs[g], x), (hs[g], hist)):
                nc.sync.dma_start(out=dst[:, j0:j1, :], in_=src[rows, :].rearrange("(p t) k -> p t k", t=GT)[:, j0:j1, :])

        def load_w(k):
            nc.sync.dma_start(out=wraw[k][:], in_=weights[k].rearrange("(p t) c -> p t c", t=4))

        def transposes(n):
            g, j = divmod(n, GT)
            tp = psum.tile([P, 4 * P], F32, name="tp%d" % j, tag="tp%d" % j)
            tps[n] = tp
            for o, src in enumerate((xs[g], hs[g])):
                words = src[:, j, :].bitcast(F32)
                for u in range(2):
                    c = (2 * o + u) * P
                    nc.tensor.transpose(tp[:, c:c + P], words[:, u:2 * P:2], ident[:])

        def leave(n, on_vector):
            g, j = divmod(n, GT)
            if g not in grps:
                grps[g] = grp_pool.tile([P, GT * 1024], BF16, name="grp", tag="grp", align_bytes=256)
            dst = grps[g][:, j * 1024:(j + 1) * 1024].bitcast(F32).rearrange("p (o b u) -> p o b u", o=2, u=2)
            src = tps[n][:].rearrange("p (o u b) -> p o b u", o=2, u=2)
            if on_vector:
                nc.vector.tensor_copy(out=dst, in_=src)
            else:
                nc.scalar.copy(out=dst, in_=src)

        def quantise(g, j0, j1):
            if g not in cods:
                cods[g] = cod_pool.tile([P, GT * 256], U32, name="cod", tag="cod", align_bytes=256)
                scls[g] = cod_pool.tile([P, GT * 256], U8, name="scl", tag="scl", align_bytes=256)
            nc.vector.quantize_mx(
                out=cods[g][:, j0 * 256:j1 * 256].bitcast(FP8X4),
                scales=scls[g][:, j0 * 256:j1 * 256],
                in_=grps[g][:, j0 * 1024:j1 * 1024],
            )

        def regroup_w(k, cv=CV):
            for c0, c1, on_vector in ((0, cv, True), (cv, D, False)):
                dst = wgrp[k][:, 4 * c0:4 * c1].rearrange("p (c i t) -> p c t i", i=4, t=4)
                src = wraw[k][:, :, c0:c1].rearrange("p t (c i) -> p c t i", i=4)
                if on_vector:
                    nc.vector.tensor_copy(out=dst, in_=src)
                else:
                    nc.scalar.copy(out=dst, in_=src)

        def quantise_w(k):
            nc.vector.quantize_mx(out=wcod[k][:].bitcast(FP8X4), scales=wscl[k][:], in_=wgrp[k][:])

        def mx(t, q, cols=(0, D)):
            g, j = divmod(t, GT)
            c0, c1 = cols
            if c0 == 0:
                r = len(banks)
                banks[(t, q)] = psum.tile([P, D], F32, name="m%d" % (r % NB), tag="m%d" % (r % NB))
            for s in range(2):
                c = j * 256 + s * P
                k = 2 * q + s
                nc.tensor.matmul_mx(
                    out=banks[(t, q)][:, c0:c1],
                    lhsT=cods[g][:, c:c + P].bitcast(FP8X4),
                    lhsT_scale=scls[g][:, c:c + P],
                    rhs=wcod[k][:, c0:c1].bitcast(FP8X4),
                    rhs_scale=wscl[k][:, c0:c1],
                    start=(s == 0),
                    stop=(s == 1),
                )

        def add_bias(t, q, cols=(0, D)):
            c0, c1 = cols
            if c0 == 0:
                pres[(t, q)] = pre_pool.tile([P, D], F32, name="a%d" % q, tag="a%d" % q)
            nc.vector.tensor_tensor(
                out=pres[(t, q)][:, c0:c1], in0=banks[(t, q)][:, c0:c1], in1=bias[:, q * D + c0:q * D + c1], op=ALU.add
            )

        def gate(t, q, cols=(0, D)):
            g, j = divmod(t, GT)
            c0, c1 = cols
            if q == 0:
                if g not in outs:
                    outs[g] = o_pool.tile([P, GT, D], F32, name="o", tag="o")
                nc.scalar.activation(out=outs[g][:, j, c0:c1], in_=pres[(t, 0)][:, c0:c1], func=ACT.Sigmoid)
            else:
                if c0 == 0:
                    tgs[t] = tg_pool.tile([P, D], F32, name="tg", tag="tg")
                nc.scalar.activation(out=tgs[t][:, c0:c1], in_=pres[(t, 1)][:, c0:c1], func=ACT.Tanh)

        def product(t, cols=(0, D)):
            g, j = divmod(t, GT)
            c0, c1 = cols
            eng = nc.vector if t in V_PRODUCTS else nc.gpsimd
            o = outs[g][:, j, c0:c1]
            eng.tensor_tensor(out=o, in0=o, in1=tgs[t][:, c0:c1], op=ALU.mult)

        def store(g, j0, j1, cols=(0, D)):
            c0, c1 = cols
            view = out[g * GT * P:(g + 1) * GT * P, :].rearrange("(p t) d -> p t d", t=GT)
            nc.sync.dma_start(out=view[:, j0:j1, c0:c1], in_=outs[g][:, j0:j1, c0:c1])

        def product_and_store(t):
            g, j = divmod(t, GT)
            product(t)
            if g == NG - 1:
                store(g, j, j + 1)
            elif j % 2 == 1:
                store(g, j - 1, j + 1)

        nc.vector.memset(ident[:], 0.0)
        make_identity(nc, ident[:], nomemset=True)
        nc.vector.memset(brow[:].bitcast(I32), 0)
        nc.vector.memset(warm[:], 0.0)
        nc.vector.memset(ones[:], 1.0)
        nc.scalar.dma_start(out=brow[0:1, 0:D], in_=b_i.rearrange("(o n) -> o n", o=1))
        nc.scalar.dma_start(out=brow[0:1, D:2 * D], in_=b_c.rearrange("(o n) -> o n", o=1))
        nc.scalar.activation(out=warm2[:], in_=warm[:], func=ACT.Sigmoid)
        load_w(0)
        load_acts(0, 0, 2)
        load_w(1)
        load_acts(0, 2, 4)
        load_w(2)
        load_acts(1, 0, 2)
        load_w(3)
        load_acts(1, 2, 4)
        for g in range(2, NG):
            load_acts(g, 0, GT)

        regroup_w(0)
        transposes(0)
        transposes(1)
        bb = psum.tile([P, 2 * D], BF16, name="bb", tag="m3")
        for q in range(2):
            nc.tensor.matmul(out=bb[:, q * D:(q + 1) * D], lhsT=ones[:], rhs=brow[:, q * D:(q + 1) * D], start=True, stop=True)
        quantise_w(0)
        leave(0, False)
        leave(1, False)
        regroup_w(1)
        quantise(0, 0, 2)
        quantise_w(1)
        transposes(2)
        transposes(3)
        mx(0, 0)
        mx(1, 0)
        leave(2, False)
        leave(3, True)
        regroup_w(2)
        nc.scalar.copy(out=bias[:], in_=bb[:])
        quantise(0, 2, 4)
        transposes(4)
        transposes(5)
        mx(2, 0)
        mx(3, 0)
        quantise_w(2)
        add_bias(0, 0)
        regroup_w(3)
        add_bias(1, 0)
        gate(0, 0)
        quantise_w(3)
        transposes(6)
        transposes(7)
        mx(0, 1)
        mx(1, 1)
        leave(4, False)
        leave(5, False)
        leave(6, False)
        add_bias(2, 0)
        gate(1, 0)
        mx(2, 1)
        add_bias(3, 0)
        gate(2, 0)
        mx(3, 1)
        leave(7, True)
        add_bias(0, 1)
        gate(0, 1)
        quantise(1, 0, 4)
        product_and_store(0)
        gate(3, 0)
        add_bias(1, 1)
        gate(1, 1)
        product_and_store(1)
        for t in (2, 3):
            add_bias(t, 1)
            gate(t, 1)
            product_and_store(t)

        for t in range(4, NT - 1):
            g, j = divmod(t, GT)
            nxt = (g + 1) * GT
            more = nxt < NT
            if j == 0 and more:
                for n in range(nxt, nxt + GT):
                    transposes(n)
            mx(t, 0)
            mx(t, 1)
            if j == 0 and more:
                leave(nxt + 0, True)
                leave(nxt + 1, False)
                leave(nxt + 2, False)
                leave(nxt + 3, False)
            add_bias(t, 0)
            add_bias(t, 1)
            if j == 1 and more:
                quantise(g + 1, 0, GT)
            gate(t, 0)
            gate(t, 1)
            if t < NT - 2:
                product_and_store(t)

        t = NT - 1
        halves = ((0, D // 2), (D // 2, D))
        mx(t, 0)
        for cols in halves:
            mx(t, 1, cols)
        add_bias(t, 0)
        gate(t, 0)
        for cols in halves:
            add_bias(t, 1, cols)
        product_and_store(t - 1)
        for cols in halves:
            gate(t, 1, cols)
            product(t, cols)
            store(NG - 1, GT - 1, GT, cols)
